import numpy as np
import ml_dtypes


def mxq(x, axis, fmt="e4m3"):
    dtype, down = {"e4m3": (ml_dtypes.float8_e4m3fn, 7), "e5m2": (ml_dtypes.float8_e5m2, 14)}[fmt]
    v = np.moveaxis(np.asarray(x, np.float32).astype(ml_dtypes.bfloat16).astype(np.float64), axis, -1)
    blocks = v.reshape(v.shape[:-1] + (-1, 32))
    amax = np.abs(blocks).max(-1, keepdims=True)
    byte = np.maximum(np.where(amax > 0, np.frexp(amax)[1] - 1 + 127, 0) - down, 1)
    scale = np.exp2(byte - 127.0)
    codes = (blocks / scale).astype(np.float32).astype(dtype).astype(np.float64)
    return np.moveaxis((codes * scale).reshape(v.shape), -1, axis)


WIDE = False


def mx_kscale(k):
    if not WIDE:
        return np.ones(k)
    levels = np.array([10, -10, 5, -5, 0])
    if k % 512:
        return np.exp2(np.random.permutation(np.resize(levels, k // 32))).repeat(32)
    a = np.empty((k // 512, 16))
    for p in range(k // 512):
        a[p, :8] = np.random.permutation(np.resize(levels, 8))
        for g in range(8):
            far = levels[np.abs(levels - a[p, g]) >= 10]
            a[p, g + 8] = far[np.random.randint(len(far))]
    return np.exp2(a.ravel()).repeat(32)


BF16 = ml_dtypes.bfloat16


def bf(x):
    return np.asarray(x, np.float32).astype(BF16)


def f64(x):
    return np.asarray(x).astype(np.float64)


B, T, D, H, HD, Q_STRIDE, WINDOW, QKV = 1, 1536, 1024, 16, 64, 4, 128, 3
NW = T // (Q_STRIDE * WINDOW)
SEQ = T // NW


def draw0():
    s = mx_kscale(D)
    return {"embeddings": bf(np.random.standard_normal((B, T, D)) * s),
            "qkv_w": bf(np.random.standard_normal((QKV * D, D)) / np.sqrt(D) / s[None, :]),
            "qkv_b": bf(np.random.standard_normal(QKV * D) * 0.3)}


def core(embeddings, qkv_w, qkv_b):
    y = (mxq(f64(embeddings), 2, "e4m3") @ mxq(f64(qkv_w), 1, "e4m3").T) + f64(qkv_b)
    qkv = y.reshape(B, SEQ, NW, QKV, H, HD)
    qkv = qkv.transpose(3, 0, 4, 2, 1, 5)
    q, k, v = qkv[0], qkv[1], qkv[2]
    q = q.reshape(B, H, NW, Q_STRIDE, SEQ // Q_STRIDE, HD).max(axis=3)
    return q, k, v


def e4m3fn_bytes(y):
    return np.clip(np.asarray(y, np.float64), -448.0, 448.0).astype(np.float32).astype(ml_dtypes.float8_e4m3fn).view(np.uint8)


def e4m3fn_values(b):
    return np.asarray(b, np.uint8).view(ml_dtypes.float8_e4m3fn).astype(np.float64)


def setup_inputs():
    d = draw0()
    x0 = np.asarray(d['qkv_w']).astype(np.float64)
    s = (np.max(np.abs(x0), axis=(0,), keepdims=True) / 448.0).astype(np.float32)
    out = {}
    for k, v in d.items():
        if k == 'qkv_w':
            out['qkv_w_bytes'] = e4m3fn_bytes(x0 / s.astype(np.float64))
            out['qkv_w_scale'] = s
        else:
            out[k] = v
    return out


def reference(embeddings, qkv_w_bytes, qkv_w_scale, qkv_b):
    return core(embeddings, e4m3fn_values(qkv_w_bytes) * qkv_w_scale.astype(np.float64), qkv_b)

@@ -1,0 +1,276 @@
+from contextlib import ExitStack
+
+import concourse.mybir as mybir
+from concourse.masks import make_identity
+
+F32 = mybir.dt.float32
+BF16 = mybir.dt.bfloat16
+U32 = mybir.dt.uint32
+U8 = mybir.dt.uint8
+FP8 = mybir.dt.float8_e4m3fn
+FP8X4 = mybir.dt.float8_e4m3fn_x4
+ADD = mybir.AluOpType.add
+MULT = mybir.AluOpType.mult
+MAX = mybir.AluOpType.max
+AX = mybir.AxisListType.X
+
+P = 128
+TOKENS, DIM, CHANNELS = 1536, 1024, 3072
+FLOPS = 2 * TOKENS * DIM * CHANNELS
+
+ORDER = (4, 5, 0, 6, 1, 7, 8, 2, 9, 3, 10, 11)
+EVAC = {0: "SSS", 1: "SSS", 3: "SVS", 5: "SSS", 6: "SVS", 8: "SSS", 10: "VSV", 11: "SVV"}
+CAST = ("V", "V", "S", "S", "S", "S", "S", "S", "S", "S", "S", "S")
+
+
+def tile_hieramaskunitattention_pa_kernel(tc, embeddings, qkv_w_bytes, qkv_w_scale, qkv_b, out_0, out_1, out_2):
+    nc = tc.nc
+    outs = (out_0, out_1, out_2)
+    with ExitStack() as ctx:
+        const = ctx.enter_context(tc.tile_pool(name="const", bufs=1))
+        castp = ctx.enter_context(tc.tile_pool(name="castp", bufs=4))
+        grp = ctx.enter_context(tc.tile_pool(name="grp", bufs=3))
+        stp = ctx.enter_context(tc.tile_pool(name="stp", bufs=8))
+        qp = ctx.enter_context(tc.tile_pool(name="qp", bufs=2))
+        psum = ctx.enter_context(tc.psum_pool(name="psum", bufs=8))
+
+        ident = const.tile([P, P], F32, name="ident")
+        make_identity(nc, ident[:])
+        sc = const.tile([P, 2, 4], F32, name="sc")
+        bias = const.tile([P, CHANNELS], BF16, name="bias")
+        xin = [const.tile([P, 2, DIM], BF16, name="xin%d" % x) for x in range(6)]
+        wbytes = [const.tile([P, 2, DIM], U8, name="wbytes%d" % a) for a in range(12)]
+        xq = [const.tile([P, 2, 256], U32, name="xq%d" % x, align_bytes=64) for x in range(6)]
+        xs = [const.tile([P, 2, 256], U8, name="xs%d" % x, align_bytes=64) for x in range(6)]
+        wq = [const.tile([P, 2, 256], U32, name="wq%d" % a, align_bytes=64) for a in range(12)]
+        ws = [const.tile([P, 2, 256], U8, name="ws%d" % a, align_bytes=64) for a in range(12)]
+
+        emb_view = embeddings.flatten_outer_dims().rearrange("(p j w) d -> w p j d", j=4, w=3)
+        wb_view = qkv_w_bytes.rearrange("(a i p) k -> a p i k", a=12, i=2)
+
+        ctx.enter_context(tc.manual_schedule())
+
+        def load_w(a):
+            nc.sync.dma_start(out=wbytes[a][:], in_=wb_view[a])
+
+        def load_x(x):
+            w, jp = x // 2, x % 2
+            nc.sync.dma_start(out=xin[x][:], in_=emb_view[w][:, 2 * jp : 2 * jp + 2, :])
+
+        load_x(0)
+        load_w(ORDER[0])
+        nc.sync.dma_start(out=sc[:], in_=qkv_w_scale.rearrange("o (g p t) -> p (o g) t", g=2, p=P, t=4))
+        load_x(1)
+        load_x(2)
+        load_w(ORDER[1])
+        load_x(3)
+        load_x(4)
+        load_w(ORDER[2])
+        load_x(5)
+        nc.sync.dma_start(out=bias[:], in_=qkv_b.partition_broadcast(P))
+        for a in ORDER[3:]:
+            load_w(a)
+
+        wcs = {}
+        banks = {}
+        wgs = {}
+        xgs = {}
+        sts = {}
+        qts = {}
+
+        def cast(n):
+            a = ORDER[n]
+            wc = castp.tile([P, 2 * DIM], BF16, name="wc", tag="wc")
+            wcs[a] = wc
+            src = wbytes[a][:].rearrange("p i k -> p (i k)").bitcast(FP8)
+            if CAST[n] == "V":
+                nc.vector.tensor_copy(out=wc[:], in_=src)
+            elif CAST[n] == "G":
+                nc.gpsimd.tensor_copy(out=wc[:], in_=src)
+            else:
+                nc.scalar.copy(out=wc[:], in_=src)
+
+        def turn(rows, key):
+            for g in range(2):
+                bank = psum.tile([P, 2, 2, P], F32, name="tbank", tag="bank")
+                banks[key + (g,)] = bank
+                for u in range(2):
+                    for i in range(2):
+                        nc.tensor.transpose(bank[:, u, i, :], rows[i][:, 256 * g + u : 256 * (g + 1) : 2], ident[:])
+
+        def tw(n):
+            a = ORDER[n]
+            turn([wcs[a][:, i * DIM : (i + 1) * DIM].bitcast(F32) for i in range(2)], ("w", a))
+
+        def aw(n, g):
+            a = ORDER[n]
+            if g == 0:
+                wgs[a] = grp.tile([P, 2, 256, 4], BF16, name="wg", tag="wg", align_bytes=64)
+            nc.vector.tensor_tensor(
+                out=wgs[a][:, g, :, :].rearrange("p c (u e) -> p c u e", u=2),
+                in0=banks[("w", a, g)][:].bitcast(BF16).rearrange("p u i (r e) -> p (i r) u e", e=2),
+                in1=sc[:, g, :].rearrange("p (u e) -> p u e", u=2).unsqueeze(1).to_broadcast([P, 256, 2, 2]),
+                op=MULT,
+            )
+
+        def quant(codes, planes, grouped):
+            nc.vector.quantize_mx(
+                out=codes[:].rearrange("p g c -> p (g c)").bitcast(FP8X4),
+                scales=planes[:].rearrange("p g c -> p (g c)"),
+                in_=grouped[:].rearrange("p g c t -> p (g c t)"),
+            )
+
+        def qw(n):
+            a = ORDER[n]
+            quant(wq[a], ws[a], wgs[a])
+
+        def tx(x):
+            turn([xin[x][:, i, :].bitcast(F32) for i in range(2)], ("x", x))
+
+        def ex(x, g, eng):
+            if g == 0:
+                xgs[x] = grp.tile([P, 2, 256, 4], BF16, name="xg", tag="xg", align_bytes=64)
+            dst = xgs[x][:].bitcast(F32)[:, g, :, :]
+            src = banks[("x", x, g)][:].rearrange("p u i r -> p (i r) u")
+            if eng == "V":
+                nc.vector.tensor_copy(out=dst, in_=src)
+            else:
+                nc.scalar.copy(out=dst, in_=src)
+
+        def qx(x):
+            quant(xq[x], xs[x], xgs[x])
+
+        def mx(out, lq, ls, rq, rs):
+            for g in range(2):
+                nc.tensor.matmul_mx(
+                    out=out,
+                    lhsT=lq[:, g, :].bitcast(FP8X4),
+                    lhsT_scale=ls[:, g, :],
+                    rhs=rq[:, g, :].bitcast(FP8X4),
+                    rhs_scale=rs[:, g, :],
+                    start=(g == 0),
+                    stop=(g == 1),
+                )
+
+        def bias_of(a):
+            return bias[:, 256 * a : 256 * (a + 1)]
+
+        def bank_kv(n, b):
+            a = ORDER[n]
+            w, jp = b // 2, b % 2
+            eng = EVAC[n][w]
+            if jp == 0:
+                sts[(a, w)] = stp.tile([P, 4, 4, 64], F32, name="st", tag="st")
+            st = sts[(a, w)]
+            acc = psum.tile([P, 2, 256], F32, name="acc", tag="bank")
+            for jj in range(2):
+                cols = slice(P * jj, P * (jj + 1))
+                mx(acc[:, jj, :], xq[b][:, :, cols], xs[b][:, :, cols], wq[a], ws[a])
+            src = acc[:].rearrange("p jj (h d) -> p jj h d", h=4)
+            dst = st[:, :, 2 * jp : 2 * jp + 2, :].rearrange("p h jj d -> p jj h d")
+            bb = bias_of(a).rearrange("p (h d) -> p h d", h=4).unsqueeze(1).to_broadcast([P, 2, 4, 64])
+            if eng == "V":
+                nc.vector.tensor_tensor(out=dst, in0=src, in1=bb, op=ADD)
+            else:
+                nc.scalar.copy(out=dst, in_=src)
+                nc.gpsimd.tensor_tensor(out=dst, in0=dst, in1=bb, op=ADD)
+            if jp == 1:
+                h0 = 4 * (a % 4)
+                to = outs[a // 4][0, h0 : h0 + 4, w].rearrange("h (p j) d -> p h (j d)", j=4)
+                nc.sync.dma_start(out=to, in_=st[:].rearrange("p h j d -> p h (j d)"))
+
+        def bank_q(n, b):
+            a = ORDER[n]
+            w, i = b // 2, b % 2
+            if b == 0:
+                qts[a] = qp.tile([P, 3, 2, P], F32, name="qt", tag="qt")
+            acc = psum.tile([P, 512], F32, name="qacc", tag="bank")
+            cols = slice(P * i, P * (i + 1))
+            for jp in range(2):
+                x = 2 * w + jp
+                mx(acc[:, 256 * jp : 256 * (jp + 1)], wq[a][:, :, cols], ws[a][:, :, cols], xq[x], xs[x])
+            nc.vector.tensor_reduce(
+                out=qts[a][:, w, i, :].rearrange("c (q j) -> c q j", j=4),
+                in_=acc[:].rearrange("c (j g q) -> c q j g", j=4, g=4),
+                axis=AX,
+                op=MAX,
+            )
+
+        def back_q(n):
+            a = ORDER[n]
+            qt = qts[a]
+            sq = qp.tile([P, 3, 256], F32, name="sq", tag="sq")
+            h0 = 4 * a
+            for w0, nw in ((0, 2), (2, 1)):
+                bank = psum.tile([P, nw, 2, P], F32, name="qbank", tag="bank")
+                for w in range(nw):
+                    for i in range(2):
+                        nc.tensor.transpose(bank[:, w, i, :], qt[:, w0 + w, i, :], ident[:])
+                dst = sq[:, w0 : w0 + nw, :]
+                nc.scalar.copy(out=dst, in_=bank[:].rearrange("p w i c -> p w (i c)"))
+                nc.gpsimd.tensor_tensor(out=dst, in0=dst, in1=bias_of(a).unsqueeze(1).to_broadcast([P, nw, 256]), op=ADD)
+                for w in range(w0, w0 + nw):
+                    nc.sync.dma_start(
+                        out=outs[0][0, h0 : h0 + 4, w].rearrange("h i d -> i h d"),
+                        in_=sq[:, w, :].rearrange("p (h d) -> p h d", h=4),
+                    )
+
+        def bank_of(n, b):
+            if ORDER[n] < 4:
+                bank_q(n, b)
+            else:
+                bank_kv(n, b)
+
+        cast(0)
+        tx(0)
+        ex(0, 0, "S")
+        ex(0, 1, "S")
+        tw(0)
+        aw(0, 0)
+        qx(0)
+        aw(0, 1)
+        tx(1)
+        ex(1, 0, "S")
+        ex(1, 1, "S")
+        cast(1)
+        qw(0)
+        tx(2)
+        ex(2, 0, "S")
+        ex(2, 1, "S")
+        qx(1)
+        tw(1)
+        aw(1, 0)
+        qx(2)
+        aw(1, 1)
+        tx(3)
+        ex(3, 0, "S")
+        ex(3, 1, "S")
+        qw(1)
+        tx(4)
+        ex(4, 0, "S")
+        ex(4, 1, "S")
+        qx(3)
+        tx(5)
+        ex(5, 0, "S")
+        ex(5, 1, "S")
+        qx(4)
+        cast(2)
+        qx(5)
+
+        for n in range(12):
+            for b in range(3):
+                bank_of(n, b)
+            if n + 3 < 12:
+                cast(n + 3)
+            if n + 2 < 12:
+                tw(n + 2)
+            if n >= 1 and ORDER[n - 1] < 4:
+                back_q(n - 1)
+            if n + 2 < 12:
+                aw(n + 2, 0)
+                aw(n + 2, 1)
+            bank_of(n, 3)
+            if n + 2 < 12:
+                qw(n + 2)
+            bank_of(n, 4)
+            bank_of(n, 5)

@@ -13,14 +13,24 @@ ADD = mybir.AluOpType.add
 MULT = mybir.AluOpType.mult
 MAX = mybir.AluOpType.max
 AX = mybir.AxisListType.X
+IDENTITY = mybir.ActivationFunctionType.Identity
 
 P = 128
 TOKENS, DIM, CHANNELS = 1536, 1024, 3072
 FLOPS = 2 * TOKENS * DIM * CHANNELS
 
-ORDER = (4, 5, 0, 6, 1, 7, 8, 2, 9, 3, 10, 11)
-EVAC = {0: "SSS", 1: "SSS", 3: "SVS", 5: "SSS", 6: "SVS", 8: "SSS", 10: "VSV", 11: "SVV"}
-CAST = ("V", "V", "S", "S", "S", "S", "S", "S", "S", "S", "S", "S")
+W_ORDER = (4, 0, 5, 6, 1, 7, 8, 2, 9, 3, 10, 11)
+OPEN = (0, 3, 8, 14, 20, 26, 32, 38, 44, 50, 56, 62)
+TW_LEAD = 7
+CAST_LEAD = 13
+QW_LAG = 2
+VBANKS = {0: (5,), 2: (2, 5), 3: (5,), 5: (2, 5), 6: (5,), 8: (2, 5), 10: (1, 3, 5), 11: (1, 3, 4, 5)}
+CAST_ENG = "VVVSSSSSSSSS"
+BIAS_LAG = 3
+BACK_LAG = 5
+MERGE = False
+HEAD = "c0 tx0 ex0 tw0 c1 a0 qx0 b0 tx1 ex1 tw1 qw0 qx1 tx2 ex2 a1 b1 qx2 s1 tx3 ex3 c2 s1 qw1 qx3 s1 tx4 ex4 s1 tw2 a2 b2 qx4 s1 tx5 ex5 s1 qw2 qx5"
+SPLIT = False
 
 
 def tile_hieramaskunitattention_pa_kernel(tc, embeddings, qkv_w_bytes, qkv_w_scale, qkv_b, out_0, out_1, out_2):
@@ -37,7 +47,8 @@ def tile_hieramaskunitattention_pa_kernel(tc, embeddings, qkv_w_bytes, qkv_w_sca
         ident = const.tile([P, P], F32, name="ident")
         make_identity(nc, ident[:])
         sc = const.tile([P, 2, 4], F32, name="sc")
-        bias = const.tile([P, CHANNELS], BF16, name="bias")
+        bias = const.tile([P, CHANNELS - DIM], BF16, name="bias")
+        bcol = const.tile([P, 8, 2], BF16, name="bcol")
         xin = [const.tile([P, 2, DIM], BF16, name="xin%d" % x) for x in range(6)]
         wbytes = [const.tile([P, 2, DIM], U8, name="wbytes%d" % a) for a in range(12)]
         xq = [const.tile([P, 2, 256], U32, name="xq%d" % x, align_bytes=64) for x in range(6)]
@@ -58,18 +69,20 @@ def tile_hieramaskunitattention_pa_kernel(tc, embeddings, qkv_w_bytes, qkv_w_sca
             nc.sync.dma_start(out=xin[x][:], in_=emb_view[w][:, 2 * jp : 2 * jp + 2, :])
 
         load_x(0)
-        load_w(ORDER[0])
+        load_w(W_ORDER[0])
         nc.sync.dma_start(out=sc[:], in_=qkv_w_scale.rearrange("o (g p t) -> p (o g) t", g=2, p=P, t=4))
         load_x(1)
+        load_w(W_ORDER[1])
         load_x(2)
-        load_w(ORDER[1])
         load_x(3)
+        load_w(W_ORDER[2])
         load_x(4)
-        load_w(ORDER[2])
         load_x(5)
-        nc.sync.dma_start(out=bias[:], in_=qkv_b.partition_broadcast(P))
-        for a in ORDER[3:]:
+        nc.sync.dma_start(out=bias[:], in_=qkv_b[DIM:CHANNELS].partition_broadcast(P))
+        for a in W_ORDER[3:]:
             load_w(a)
+        with nc.allow_non_contiguous_dma(reason="one bias value to a partition"):
+            nc.sync.dma_start(out=bcol[:, :, 0], in_=qkv_b[0:DIM].rearrange("(t p) -> p t", p=P))
 
         wcs = {}
         banks = {}
@@ -78,14 +91,14 @@ def tile_hieramaskunitattention_pa_kernel(tc, embeddings, qkv_w_bytes, qkv_w_sca
         sts = {}
         qts = {}
 
-        def cast(n):
-            a = ORDER[n]
+        def cast(k):
+            a = W_ORDER[k]
             wc = castp.tile([P, 2 * DIM], BF16, name="wc", tag="wc")
             wcs[a] = wc
             src = wbytes[a][:].rearrange("p i k -> p (i k)").bitcast(FP8)
-            if CAST[n] == "V":
+            if CAST_ENG[k] == "V":
                 nc.vector.tensor_copy(out=wc[:], in_=src)
-            elif CAST[n] == "G":
+            elif CAST_ENG[k] == "G":
                 nc.gpsimd.tensor_copy(out=wc[:], in_=src)
             else:
                 nc.scalar.copy(out=wc[:], in_=src)
@@ -98,12 +111,12 @@ def tile_hieramaskunitattention_pa_kernel(tc, embeddings, qkv_w_bytes, qkv_w_sca
                     for i in range(2):
                         nc.tensor.transpose(bank[:, u, i, :], rows[i][:, 256 * g + u : 256 * (g + 1) : 2], ident[:])
 
-        def tw(n):
-            a = ORDER[n]
+        def tw(k):
+            a = W_ORDER[k]
             turn([wcs[a][:, i * DIM : (i + 1) * DIM].bitcast(F32) for i in range(2)], ("w", a))
 
-        def aw(n, g):
-            a = ORDER[n]
+        def aw(k, g):
+            a = W_ORDER[k]
             if g == 0:
                 wgs[a] = grp.tile([P, 2, 256, 4], BF16, name="wg", tag="wg", align_bytes=64)
             nc.vector.tensor_tensor(
@@ -120,8 +133,8 @@ def tile_hieramaskunitattention_pa_kernel(tc, embeddings, qkv_w_bytes, qkv_w_sca
                 in_=grouped[:].rearrange("p g c t -> p (g c t)"),
             )
 
-        def qw(n):
-            a = ORDER[n]
+        def qw(k):
+            a = W_ORDER[k]
             quant(wq[a], ws[a], wgs[a])
 
         def tx(x):
@@ -153,12 +166,12 @@ def tile_hieramaskunitattention_pa_kernel(tc, embeddings, qkv_w_bytes, qkv_w_sca
                 )
 
         def bias_of(a):
-            return bias[:, 256 * a : 256 * (a + 1)]
+            return bias[:, 256 * (a - 4) : 256 * (a - 3)]
 
-        def bank_kv(n, b):
-            a = ORDER[n]
+        def bank_kv(k, b):
+            a = W_ORDER[k]
             w, jp = b // 2, b % 2
-            eng = EVAC[n][w]
+            eng = "V" if b in VBANKS[k] else "S"
             if jp == 0:
                 sts[(a, w)] = stp.tile([P, 4, 4, 64], F32, name="st", tag="st")
             st = sts[(a, w)]
@@ -173,14 +186,22 @@ def tile_hieramaskunitattention_pa_kernel(tc, embeddings, qkv_w_bytes, qkv_w_sca
                 nc.vector.tensor_tensor(out=dst, in0=src, in1=bb, op=ADD)
             else:
                 nc.scalar.copy(out=dst, in_=src)
-                nc.gpsimd.tensor_tensor(out=dst, in0=dst, in1=bb, op=ADD)
+                both = MERGE and (2 * w) not in VBANKS[k] and (2 * w + 1) not in VBANKS[k]
+                if SPLIT:
+                    for jj in range(2):
+                        nc.gpsimd.tensor_tensor(out=dst[:, jj], in0=dst[:, jj], in1=bb[:, jj], op=ADD)
+                elif not both:
+                    nc.gpsimd.tensor_tensor(out=dst, in0=dst, in1=bb, op=ADD)
+                elif jp == 1:
+                    b4 = bias_of(a).rearrange("p (h d) -> p h d", h=4).unsqueeze(2).to_broadcast([P, 4, 4, 64])
+                    nc.gpsimd.tensor_tensor(out=st[:], in0=st[:], in1=b4, op=ADD)
             if jp == 1:
                 h0 = 4 * (a % 4)
                 to = outs[a // 4][0, h0 : h0 + 4, w].rearrange("h (p j) d -> p h (j d)", j=4)
                 nc.sync.dma_start(out=to, in_=st[:].rearrange("p h j d -> p h (j d)"))
 
-        def bank_q(n, b):
-            a = ORDER[n]
+        def bank_q(k, b):
+            a = W_ORDER[k]
             w, i = b // 2, b % 2
             if b == 0:
                 qts[a] = qp.tile([P, 3, 2, P], F32, name="qt", tag="qt")
@@ -196,8 +217,13 @@ def tile_hieramaskunitattention_pa_kernel(tc, embeddings, qkv_w_bytes, qkv_w_sca
                 op=MAX,
             )
 
-        def back_q(n):
-            a = ORDER[n]
+        def bias_q(k):
+            a = W_ORDER[k]
+            for i in range(2):
+                nc.scalar.activation(out=qts[a][:, :, i, :], in_=qts[a][:, :, i, :], func=IDENTITY, bias=bcol[:, 2 * a + i, 0:1], scale=1.0)
+
+        def back_q(k):
+            a = W_ORDER[k]
             qt = qts[a]
             sq = qp.tile([P, 3, 256], F32, name="sq", tag="sq")
             h0 = 4 * a
@@ -208,69 +234,92 @@ def tile_hieramaskunitattention_pa_kernel(tc, embeddings, qkv_w_bytes, qkv_w_sca
                         nc.tensor.transpose(bank[:, w, i, :], qt[:, w0 + w, i, :], ident[:])
                 dst = sq[:, w0 : w0 + nw, :]
                 nc.scalar.copy(out=dst, in_=bank[:].rearrange("p w i c -> p w (i c)"))
-                nc.gpsimd.tensor_tensor(out=dst, in0=dst, in1=bias_of(a).unsqueeze(1).to_broadcast([P, nw, 256]), op=ADD)
                 for w in range(w0, w0 + nw):
                     nc.sync.dma_start(
                         out=outs[0][0, h0 : h0 + 4, w].rearrange("h i d -> i h d"),
                         in_=sq[:, w, :].rearrange("p (h d) -> p h d", h=4),
                     )
 
-        def bank_of(n, b):
-            if ORDER[n] < 4:
-                bank_q(n, b)
+        stream = []
+        done = [0] * 12
+        prev = 0
+        while len(stream) < 72:
+            ks = [k for k in range(12) if OPEN[k] <= len(stream) and done[k] < 6]
+            later = [k for k in ks if k > prev]
+            k = later[0] if later else ks[0]
+            prev = k
+            stream.append((k, done[k]))
+            done[k] += 1
+
+        hooks = {}
+
+        def at(slot, what):
+            hooks.setdefault(max(slot, 0), []).append(what)
+
+        first = {}
+        last = {}
+        for t, (k, b) in enumerate(stream):
+            first.setdefault(k, t)
+            last[k] = t
+        for k in range(3, 12):
+            at(first[k] - CAST_LEAD, ("cast", k))
+            at(first[k] - TW_LEAD, ("tw", k))
+            at(first[k] - TW_LEAD + QW_LAG, ("qw", k))
+        for k in range(12):
+            if W_ORDER[k] < 4:
+                at(last[k] + BIAS_LAG, ("bias", k))
+                at(last[k] + BACK_LAG, ("back", k))
+
+        def run(what, k):
+            if what == "cast":
+                cast(k)
+            elif what == "tw":
+                tw(k)
+                aw(k, 0)
+                aw(k, 1)
+            elif what == "qw":
+                qw(k)
+            elif what == "bias":
+                bias_q(k)
             else:
-                bank_kv(n, b)
+                back_q(k)
 
-        cast(0)
-        tx(0)
-        ex(0, 0, "S")
-        ex(0, 1, "S")
-        tw(0)
-        aw(0, 0)
-        qx(0)
-        aw(0, 1)
-        tx(1)
-        ex(1, 0, "S")
-        ex(1, 1, "S")
-        cast(1)
-        qw(0)
-        tx(2)
-        ex(2, 0, "S")
-        ex(2, 1, "S")
-        qx(1)
-        tw(1)
-        aw(1, 0)
-        qx(2)
-        aw(1, 1)
-        tx(3)
-        ex(3, 0, "S")
-        ex(3, 1, "S")
-        qw(1)
-        tx(4)
-        ex(4, 0, "S")
-        ex(4, 1, "S")
-        qx(3)
-        tx(5)
-        ex(5, 0, "S")
-        ex(5, 1, "S")
-        qx(4)
-        cast(2)
-        qx(5)
+        def slot(t):
+            order = {"cast": 0, "bias": 1, "tw": 2, "back": 3, "qw": 4}
+            for what, k in sorted(hooks.get(t, []), key=lambda h: order[h[0]]):
+                run(what, k)
+            if t < 72:
+                k, b = stream[t]
+                if W_ORDER[k] < 4:
+                    bank_q(k, b)
+                else:
+                    bank_kv(k, b)
 
-        for n in range(12):
-            for b in range(3):
-                bank_of(n, b)
-            if n + 3 < 12:
-                cast(n + 3)
-            if n + 2 < 12:
-                tw(n + 2)
-            if n >= 1 and ORDER[n - 1] < 4:
-                back_q(n - 1)
-            if n + 2 < 12:
-                aw(n + 2, 0)
-                aw(n + 2, 1)
-            bank_of(n, 3)
-            if n + 2 < 12:
-                qw(n + 2)
-            bank_of(n, 4)
-            bank_of(n, 5)
+        t = 0
+        for tok in HEAD.split():
+            n = int(tok[-1])
+            op = tok[:-1]
+            if op == "c":
+                cast(n)
+            elif op == "tx":
+                tx(n)
+            elif op == "ex":
+                ex(n, 0, "S")
+                ex(n, 1, "S")
+            elif op == "qx":
+                qx(n)
+            elif op == "tw":
+                tw(n)
+            elif op == "a":
+                aw(n, 0)
+            elif op == "b":
+                aw(n, 1)
+            elif op == "qw":
+                qw(n)
+            else:
+                for r in range(n):
+                    slot(t)
+                    t += 1
+        while t < 72 + 8:
+            slot(t)
+            t += 1

@@ -19,17 +19,23 @@ P = 128
 TOKENS, DIM, CHANNELS = 1536, 1024, 3072
 FLOPS = 2 * TOKENS * DIM * CHANNELS
 
-W_ORDER = (4, 0, 5, 6, 1, 7, 8, 2, 9, 3, 10, 11)
-OPEN = (0, 3, 8, 14, 20, 26, 32, 38, 44, 50, 56, 62)
+W_ORDER = (4, 0, 5, 6, 1, 7, 8, 2, 9, 10, 3, 11)
+OPEN = (0, 1, 10, 16, 22, 28, 34, 40, 46, 52, 58, 64)
 TW_LEAD = 7
 CAST_LEAD = 13
 QW_LAG = 2
-VBANKS = {0: (5,), 2: (2, 5), 3: (5,), 5: (2, 5), 6: (5,), 8: (2, 5), 10: (1, 3, 5), 11: (1, 3, 4, 5)}
-CAST_ENG = "VVVSSSSSSSSS"
-BIAS_LAG = 3
+VB_EVEN = (5,)
+VB_ODD = (2, 5)
+VB_END = {10: (1, 3, 5), 11: (1, 3, 4, 5)}
+KV_POS = [k for k in range(12) if W_ORDER[k] >= 4]
+VBANKS = dict((k, VB_END.get(k, VB_ODD if n % 2 else VB_EVEN)) for n, k in enumerate(KV_POS))
+CAST_ENG = "VVSSSSSSSSSS"
+BIAS_LEAD = 2
 BACK_LAG = 5
+JOIN = True
+NHEAD = 2
 MERGE = False
-HEAD = "c0 tx0 ex0 tw0 c1 a0 qx0 b0 tx1 ex1 tw1 qw0 qx1 tx2 ex2 a1 b1 qx2 s1 tx3 ex3 c2 s1 qw1 qx3 s1 tx4 ex4 s1 tw2 a2 b2 qx4 s1 tx5 ex5 s1 qw2 qx5"
+HEAD = "c0 tx0 ex0 tw0 c1 a0 qx0 b0 tx1 ex1 qw0 qx1 tx2 ex2 tw1 a1 b1 qx2 tx3 ex3 qw1 qx3 tx4 ex4 qx4 tx5 ex5 qx5"
 SPLIT = False
 
 
@@ -261,14 +267,17 @@ def tile_hieramaskunitattention_pa_kernel(tc, embeddings, qkv_w_bytes, qkv_w_sca
         for t, (k, b) in enumerate(stream):
             first.setdefault(k, t)
             last[k] = t
-        for k in range(3, 12):
+        for k in range(NHEAD, 12):
             at(first[k] - CAST_LEAD, ("cast", k))
             at(first[k] - TW_LEAD, ("tw", k))
             at(first[k] - TW_LEAD + QW_LAG, ("qw", k))
+        tw_slots = sorted(first[k] - TW_LEAD for k in range(NHEAD, 12))
         for k in range(12):
             if W_ORDER[k] < 4:
-                at(last[k] + BIAS_LAG, ("bias", k))
-                at(last[k] + BACK_LAG, ("back", k))
+                later_runs = [s for s in tw_slots if s >= last[k] + BACK_LAG] if JOIN else []
+                back_at = later_runs[0] if later_runs else last[k] + BACK_LAG
+                at(back_at - BIAS_LEAD, ("bias", k))
+                at(back_at, ("back", k))
 
         def run(what, k):
             if what == "cast":

@@ -33,7 +33,12 @@ CAST_ENG = "VVSSSSSSSSSS"
 BIAS_LEAD = 2
 BACK_LAG = 5
 JOIN = True
+LAST_BACK_LAG = 5
 NHEAD = 2
+XG_BUFS = 6
+RUN = 1
+AW_STEP = 3
+CAST_STEP = 4
 MERGE = False
 HEAD = "c0 tx0 ex0 tw0 c1 a0 qx0 b0 tx1 ex1 qw0 qx1 tx2 ex2 tw1 a1 b1 qx2 tx3 ex3 qw1 qx3 tx4 ex4 qx4 tx5 ex5 qx5"
 SPLIT = False
@@ -46,6 +51,7 @@ def tile_hieramaskunitattention_pa_kernel(tc, embeddings, qkv_w_bytes, qkv_w_sca
         const = ctx.enter_context(tc.tile_pool(name="const", bufs=1))
         castp = ctx.enter_context(tc.tile_pool(name="castp", bufs=4))
         grp = ctx.enter_context(tc.tile_pool(name="grp", bufs=3))
+        xgp = ctx.enter_context(tc.tile_pool(name="xgp", bufs=XG_BUFS))
         stp = ctx.enter_context(tc.tile_pool(name="stp", bufs=8))
         qp = ctx.enter_context(tc.tile_pool(name="qp", bufs=2))
         psum = ctx.enter_context(tc.psum_pool(name="psum", bufs=8))
@@ -148,7 +154,7 @@ def tile_hieramaskunitattention_pa_kernel(tc, embeddings, qkv_w_bytes, qkv_w_sca
 
         def ex(x, g, eng):
             if g == 0:
-                xgs[x] = grp.tile([P, 2, 256, 4], BF16, name="xg", tag="xg", align_bytes=64)
+                xgs[x] = xgp.tile([P, 2, 256, 4], BF16, name="xg", tag="xg", align_bytes=64)
             dst = xgs[x][:].bitcast(F32)[:, g, :, :]
             src = banks[("x", x, g)][:].rearrange("p u i r -> p (i r) u")
             if eng == "V":
@@ -268,14 +274,19 @@ def tile_hieramaskunitattention_pa_kernel(tc, embeddings, qkv_w_bytes, qkv_w_sca
             first.setdefault(k, t)
             last[k] = t
         for k in range(NHEAD, 12):
-            at(first[k] - CAST_LEAD, ("cast", k))
-            at(first[k] - TW_LEAD, ("tw", k))
-            at(first[k] - TW_LEAD + QW_LAG, ("qw", k))
-        tw_slots = sorted(first[k] - TW_LEAD for k in range(NHEAD, 12))
+            lead = k - (k - NHEAD) % RUN
+            run_at = first[lead] - TW_LEAD
+            m = k - lead
+            if ("c%d" % k) not in HEAD.split():
+                at(run_at - (CAST_LEAD - TW_LEAD) - CAST_STEP * (RUN - 1 - m), ("cast", k))
+            at(run_at, ("tw", k))
+            at(run_at + AW_STEP * m, ("aw", k))
+            at(run_at + AW_STEP * m + QW_LAG, ("qw", k))
+        tw_slots = sorted(first[k] - TW_LEAD for k in range(NHEAD, 12, RUN))
         for k in range(12):
             if W_ORDER[k] < 4:
                 later_runs = [s for s in tw_slots if s >= last[k] + BACK_LAG] if JOIN else []
-                back_at = later_runs[0] if later_runs else last[k] + BACK_LAG
+                back_at = later_runs[0] if later_runs else last[k] + LAST_BACK_LAG
                 at(back_at - BIAS_LEAD, ("bias", k))
                 at(back_at, ("back", k))
 
@@ -284,6 +295,7 @@ def tile_hieramaskunitattention_pa_kernel(tc, embeddings, qkv_w_bytes, qkv_w_sca
                 cast(k)
             elif what == "tw":
                 tw(k)
+            elif what == "aw":
                 aw(k, 0)
                 aw(k, 1)
             elif what == "qw":
@@ -294,7 +306,7 @@ def tile_hieramaskunitattention_pa_kernel(tc, embeddings, qkv_w_bytes, qkv_w_sca
                 back_q(k)
 
         def slot(t):
-            order = {"cast": 0, "bias": 1, "tw": 2, "back": 3, "qw": 4}
+            order = {"cast": 0, "bias": 1, "tw": 2, "back": 3, "aw": 4, "qw": 5}
             for what, k in sorted(hooks.get(t, []), key=lambda h: order[h[0]]):
                 run(what, k)
             if t < 72:

@@ -34,13 +34,13 @@ BIAS_LEAD = 2
 BACK_LAG = 5
 JOIN = True
 LAST_BACK_LAG = 5
-NHEAD = 2
+NHEAD = 3
 XG_BUFS = 6
 RUN = 1
 AW_STEP = 3
 CAST_STEP = 4
 MERGE = False
-HEAD = "c0 tx0 ex0 tw0 c1 a0 qx0 b0 tx1 ex1 qw0 qx1 tx2 ex2 tw1 a1 b1 qx2 tx3 ex3 qw1 qx3 tx4 ex4 qx4 tx5 ex5 qx5"
+HEAD = "c0 tx0 ex0 tw0 c1 a0 qx0 b0 tx1 ex1 qw0 qx1 tx2 ex2 c2 tw1 a1 b1 qx2 tx3 ex3 qw1 qx3 tx4 ex4 qx4 tx5 ex5 tw2 qx5 a2 b2 s2 qw2"
 SPLIT = False
 
 

@@ -24,8 +24,8 @@ OPEN = (0, 1, 10, 16, 22, 28, 34, 40, 46, 52, 58, 64)
 TW_LEAD = 7
 CAST_LEAD = 13
 QW_LAG = 2
-VB_EVEN = (5,)
-VB_ODD = (2, 5)
+VB_EVEN = (2,)
+VB_ODD = (3, 5)
 VB_END = {10: (1, 3, 5), 11: (1, 3, 4, 5)}
 KV_POS = [k for k in range(12) if W_ORDER[k] >= 4]
 VBANKS = dict((k, VB_END.get(k, VB_ODD if n % 2 else VB_EVEN)) for n, k in enumerate(KV_POS))

from contextlib import ExitStack

import concourse.mybir as mybir
from concourse.masks import make_identity

F32 = mybir.dt.float32
BF16 = mybir.dt.bfloat16
U32 = mybir.dt.uint32
U8 = mybir.dt.uint8
FP8 = mybir.dt.float8_e4m3fn
FP8X4 = mybir.dt.float8_e4m3fn_x4
ADD = mybir.AluOpType.add
MULT = mybir.AluOpType.mult
MAX = mybir.AluOpType.max
AX = mybir.AxisListType.X
IDENTITY = mybir.ActivationFunctionType.Identity

P = 128
TOKENS, DIM, CHANNELS = 1536, 1024, 3072
FLOPS = 2 * TOKENS * DIM * CHANNELS

W_ORDER = (4, 0, 5, 6, 1, 7, 8, 2, 9, 10, 3, 11)
OPEN = (0, 1, 10, 16, 22, 28, 34, 40, 46, 52, 58, 64)
TW_LEAD = 7
CAST_LEAD = 13
QW_LAG = 2
VB_EVEN = (2,)
VB_ODD = (3, 5)
VB_END = {10: (1, 3, 5), 11: (1, 3, 4, 5)}
KV_POS = [k for k in range(12) if W_ORDER[k] >= 4]
VBANKS = dict((k, VB_END.get(k, VB_ODD if n % 2 else VB_EVEN)) for n, k in enumerate(KV_POS))
CAST_ENG = "VVSSSSSSSSSS"
BIAS_LEAD = 2
BACK_LAG = 5
JOIN = True
LAST_BACK_LAG = 5
NHEAD = 3
XG_BUFS = 6
RUN = 1
AW_STEP = 3
CAST_STEP = 4
MERGE = False
HEAD = "c0 tx0 ex0 tw0 c1 a0 qx0 b0 tx1 ex1 qw0 qx1 tx2 ex2 c2 tw1 a1 b1 qx2 tx3 ex3 qw1 qx3 tx4 ex4 qx4 tx5 ex5 tw2 qx5 a2 b2 s2 qw2"
SPLIT = False


def tile_hieramaskunitattention_pa_kernel(tc, embeddings, qkv_w_bytes, qkv_w_scale, qkv_b, out_0, out_1, out_2):
    nc = tc.nc
    outs = (out_0, out_1, out_2)
    with ExitStack() as ctx:
        const = ctx.enter_context(tc.tile_pool(name="const", bufs=1))
        castp = ctx.enter_context(tc.tile_pool(name="castp", bufs=4))
        grp = ctx.enter_context(tc.tile_pool(name="grp", bufs=3))
        xgp = ctx.enter_context(tc.tile_pool(name="xgp", bufs=XG_BUFS))
        stp = ctx.enter_context(tc.tile_pool(name="stp", bufs=8))
        qp = ctx.enter_context(tc.tile_pool(name="qp", bufs=2))
        psum = ctx.enter_context(tc.psum_pool(name="psum", bufs=8))

        ident = const.tile([P, P], F32, name="ident")
        make_identity(nc, ident[:])
        sc = const.tile([P, 2, 4], F32, name="sc")
        bias = const.tile([P, CHANNELS - DIM], BF16, name="bias")
        bcol = const.tile([P, 8, 2], BF16, name="bcol")
        xin = [const.tile([P, 2, DIM], BF16, name="xin%d" % x) for x in range(6)]
        wbytes = [const.tile([P, 2, DIM], U8, name="wbytes%d" % a) for a in range(12)]
        xq = [const.tile([P, 2, 256], U32, name="xq%d" % x, align_bytes=64) for x in range(6)]
        xs = [const.tile([P, 2, 256], U8, name="xs%d" % x, align_bytes=64) for x in range(6)]
        wq = [const.tile([P, 2, 256], U32, name="wq%d" % a, align_bytes=64) for a in range(12)]
        ws = [const.tile([P, 2, 256], U8, name="ws%d" % a, align_bytes=64) for a in range(12)]

        emb_view = embeddings.flatten_outer_dims().rearrange("(p j w) d -> w p j d", j=4, w=3)
        wb_view = qkv_w_bytes.rearrange("(a i p) k -> a p i k", a=12, i=2)

        ctx.enter_context(tc.manual_schedule())

        def load_w(a):
            nc.sync.dma_start(out=wbytes[a][:], in_=wb_view[a])

        def load_x(x):
            w, jp = x // 2, x % 2
            nc.sync.dma_start(out=xin[x][:], in_=emb_view[w][:, 2 * jp : 2 * jp + 2, :])

        load_x(0)
        load_w(W_ORDER[0])
        nc.sync.dma_start(out=sc[:], in_=qkv_w_scale.rearrange("o (g p t) -> p (o g) t", g=2, p=P, t=4))
        load_x(1)
        load_w(W_ORDER[1])
        load_x(2)
        load_x(3)
        load_w(W_ORDER[2])
        load_x(4)
        load_x(5)
        nc.sync.dma_start(out=bias[:], in_=qkv_b[DIM:CHANNELS].partition_broadcast(P))
        for a in W_ORDER[3:]:
            load_w(a)
        with nc.allow_non_contiguous_dma(reason="one bias value to a partition"):
            nc.sync.dma_start(out=bcol[:, :, 0], in_=qkv_b[0:DIM].rearrange("(t p) -> p t", p=P))

        wcs = {}
        banks = {}
        wgs = {}
        xgs = {}
        sts = {}
        qts = {}

        def cast(k):
            a = W_ORDER[k]
            wc = castp.tile([P, 2 * DIM], BF16, name="wc", tag="wc")
            wcs[a] = wc
            src = wbytes[a][:].rearrange("p i k -> p (i k)").bitcast(FP8)
            if CAST_ENG[k] == "V":
                nc.vector.tensor_copy(out=wc[:], in_=src)
            elif CAST_ENG[k] == "G":
                nc.gpsimd.tensor_copy(out=wc[:], in_=src)
            else:
                nc.scalar.copy(out=wc[:], in_=src)

        def turn(rows, key):
            for g in range(2):
                bank = psum.tile([P, 2, 2, P], F32, name="tbank", tag="bank")
                banks[key + (g,)] = bank
                for u in range(2):
                    for i in range(2):
                        nc.tensor.transpose(bank[:, u, i, :], rows[i][:, 256 * g + u : 256 * (g + 1) : 2], ident[:])

        def tw(k):
            a = W_ORDER[k]
            turn([wcs[a][:, i * DIM : (i + 1) * DIM].bitcast(F32) for i in range(2)], ("w", a))

        def aw(k, g):
            a = W_ORDER[k]
            if g == 0:
                wgs[a] = grp.tile([P, 2, 256, 4], BF16, name="wg", tag="wg", align_bytes=64)
            nc.vector.tensor_tensor(
                out=wgs[a][:, g, :, :].rearrange("p c (u e) -> p c u e", u=2),
                in0=banks[("w", a, g)][:].bitcast(BF16).rearrange("p u i (r e) -> p (i r) u e", e=2),
                in1=sc[:, g, :].rearrange("p (u e) -> p u e", u=2).unsqueeze(1).to_broadcast([P, 256, 2, 2]),
                op=MULT,
            )

        def quant(codes, planes, grouped):
            nc.vector.quantize_mx(
                out=codes[:].rearrange("p g c -> p (g c)").bitcast(FP8X4),
                scales=planes[:].rearrange("p g c -> p (g c)"),
                in_=grouped[:].rearrange("p g c t -> p (g c t)"),
            )

        def qw(k):
            a = W_ORDER[k]
            quant(wq[a], ws[a], wgs[a])

        def tx(x):
            turn([xin[x][:, i, :].bitcast(F32) for i in range(2)], ("x", x))

        def ex(x, g, eng):
            if g == 0:
                xgs[x] = xgp.tile([P, 2, 256, 4], BF16, name="xg", tag="xg", align_bytes=64)
            dst = xgs[x][:].bitcast(F32)[:, g, :, :]
            src = banks[("x", x, g)][:].rearrange("p u i r -> p (i r) u")
            if eng == "V":
                nc.vector.tensor_copy(out=dst, in_=src)
            else:
                nc.scalar.copy(out=dst, in_=src)

        def qx(x):
            quant(xq[x], xs[x], xgs[x])

        def mx(out, lq, ls, rq, rs):
            for g in range(2):
                nc.tensor.matmul_mx(
                    out=out,
                    lhsT=lq[:, g, :].bitcast(FP8X4),
                    lhsT_scale=ls[:, g, :],
                    rhs=rq[:, g, :].bitcast(FP8X4),
                    rhs_scale=rs[:, g, :],
                    start=(g == 0),
                    stop=(g == 1),
                )

        def bias_of(a):
            return bias[:, 256 * (a - 4) : 256 * (a - 3)]

        def bank_kv(k, b):
            a = W_ORDER[k]
            w, jp = b // 2, b % 2
            eng = "V" if b in VBANKS[k] else "S"
            if jp == 0:
                sts[(a, w)] = stp.tile([P, 4, 4, 64], F32, name="st", tag="st")
            st = sts[(a, w)]
            acc = psum.tile([P, 2, 256], F32, name="acc", tag="bank")
            for jj in range(2):
                cols = slice(P * jj, P * (jj + 1))
                mx(acc[:, jj, :], xq[b][:, :, cols], xs[b][:, :, cols], wq[a], ws[a])
            src = acc[:].rearrange("p jj (h d) -> p jj h d", h=4)
            dst = st[:, :, 2 * jp : 2 * jp + 2, :].rearrange("p h jj d -> p jj h d")
            bb = bias_of(a).rearrange("p (h d) -> p h d", h=4).unsqueeze(1).to_broadcast([P, 2, 4, 64])
            if eng == "V":
                nc.vector.tensor_tensor(out=dst, in0=src, in1=bb, op=ADD)
            else:
                nc.scalar.copy(out=dst, in_=src)
                both = MERGE and (2 * w) not in VBANKS[k] and (2 * w + 1) not in VBANKS[k]
                if SPLIT:
                    for jj in range(2):
                        nc.gpsimd.tensor_tensor(out=dst[:, jj], in0=dst[:, jj], in1=bb[:, jj], op=ADD)
                elif not both:
                    nc.gpsimd.tensor_tensor(out=dst, in0=dst, in1=bb, op=ADD)
                elif jp == 1:
                    b4 = bias_of(a).rearrange("p (h d) -> p h d", h=4).unsqueeze(2).to_broadcast([P, 4, 4, 64])
                    nc.gpsimd.tensor_tensor(out=st[:], in0=st[:], in1=b4, op=ADD)
            if jp == 1:
                h0 = 4 * (a % 4)
                to = outs[a // 4][0, h0 : h0 + 4, w].rearrange("h (p j) d -> p h (j d)", j=4)
                nc.sync.dma_start(out=to, in_=st[:].rearrange("p h j d -> p h (j d)"))

        def bank_q(k, b):
            a = W_ORDER[k]
            w, i = b // 2, b % 2
            if b == 0:
                qts[a] = qp.tile([P, 3, 2, P], F32, name="qt", tag="qt")
            acc = psum.tile([P, 512], F32, name="qacc", tag="bank")
            cols = slice(P * i, P * (i + 1))
            for jp in range(2):
                x = 2 * w + jp
                mx(acc[:, 256 * jp : 256 * (jp + 1)], wq[a][:, :, cols], ws[a][:, :, cols], xq[x], xs[x])
            nc.vector.tensor_reduce(
                out=qts[a][:, w, i, :].rearrange("c (q j) -> c q j", j=4),
                in_=acc[:].rearrange("c (j g q) -> c q j g", j=4, g=4),
                axis=AX,
                op=MAX,
            )

        def bias_q(k):
            a = W_ORDER[k]
            for i in range(2):
                nc.scalar.activation(out=qts[a][:, :, i, :], in_=qts[a][:, :, i, :], func=IDENTITY, bias=bcol[:, 2 * a + i, 0:1], scale=1.0)

        def back_q(k):
            a = W_ORDER[k]
            qt = qts[a]
            sq = qp.tile([P, 3, 256], F32, name="sq", tag="sq")
            h0 = 4 * a
            for w0, nw in ((0, 2), (2, 1)):
                bank = psum.tile([P, nw, 2, P], F32, name="qbank", tag="bank")
                for w in range(nw):
                    for i in range(2):
                        nc.tensor.transpose(bank[:, w, i, :], qt[:, w0 + w, i, :], ident[:])
                dst = sq[:, w0 : w0 + nw, :]
                nc.scalar.copy(out=dst, in_=bank[:].rearrange("p w i c -> p w (i c)"))
                for w in range(w0, w0 + nw):
                    nc.sync.dma_start(
                        out=outs[0][0, h0 : h0 + 4, w].rearrange("h i d -> i h d"),
                        in_=sq[:, w, :].rearrange("p (h d) -> p h d", h=4),
                    )

        stream = []
        done = [0] * 12
        prev = 0
        while len(stream) < 72:
            ks = [k for k in range(12) if OPEN[k] <= len(stream) and done[k] < 6]
            later = [k for k in ks if k > prev]
            k = later[0] if later else ks[0]
            prev = k
            stream.append((k, done[k]))
            done[k] += 1

        hooks = {}

        def at(slot, what):
            hooks.setdefault(max(slot, 0), []).append(what)

        first = {}
        last = {}
        for t, (k, b) in enumerate(stream):
            first.setdefault(k, t)
            last[k] = t
        for k in range(NHEAD, 12):
            lead = k - (k - NHEAD) % RUN
            run_at = first[lead] - TW_LEAD
            m = k - lead
            if ("c%d" % k) not in HEAD.split():
                at(run_at - (CAST_LEAD - TW_LEAD) - CAST_STEP * (RUN - 1 - m), ("cast", k))
            at(run_at, ("tw", k))
            at(run_at + AW_STEP * m, ("aw", k))
            at(run_at + AW_STEP * m + QW_LAG, ("qw", k))
        tw_slots = sorted(first[k] - TW_LEAD for k in range(NHEAD, 12, RUN))
        for k in range(12):
            if W_ORDER[k] < 4:
                later_runs = [s for s in tw_slots if s >= last[k] + BACK_LAG] if JOIN else []
                back_at = later_runs[0] if later_runs else last[k] + LAST_BACK_LAG
                at(back_at - BIAS_LEAD, ("bias", k))
                at(back_at, ("back", k))

        def run(what, k):
            if what == "cast":
                cast(k)
            elif what == "tw":
                tw(k)
            elif what == "aw":
                aw(k, 0)
                aw(k, 1)
            elif what == "qw":
                qw(k)
            elif what == "bias":
                bias_q(k)
            else:
                back_q(k)

        def slot(t):
            order = {"cast": 0, "bias": 1, "tw": 2, "back": 3, "aw": 4, "qw": 5}
            for what, k in sorted(hooks.get(t, []), key=lambda h: order[h[0]]):
                run(what, k)
            if t < 72:
                k, b = stream[t]
                if W_ORDER[k] < 4:
                    bank_q(k, b)
                else:
                    bank_kv(k, b)

        t = 0
        for tok in HEAD.split():
            n = int(tok[-1])
            op = tok[:-1]
            if op == "c":
                cast(n)
            elif op == "tx":
                tx(n)
            elif op == "ex":
                ex(n, 0, "S")
                ex(n, 1, "S")
            elif op == "qx":
                qx(n)
            elif op == "tw":
                tw(n)
            elif op == "a":
                aw(n, 0)
            elif op == "b":
                aw(n, 1)
            elif op == "qw":
                qw(n)
            else:
                for r in range(n):
                    slot(t)
                    t += 1
        while t < 72 + 8:
            slot(t)
            t += 1
